import numpy as np
import ml_dtypes


def mxq(x, axis, fmt="e4m3"):
    dtype, down = {"e4m3": (ml_dtypes.float8_e4m3fn, 7), "e5m2": (ml_dtypes.float8_e5m2, 14)}[fmt]
    v = np.moveaxis(np.asarray(x, np.float32).astype(ml_dtypes.bfloat16).astype(np.float64), axis, -1)
    blocks = v.reshape(v.shape[:-1] + (-1, 32))
    amax = np.abs(blocks).max(-1, keepdims=True)
    byte = np.maximum(np.where(amax > 0, np.frexp(amax)[1] - 1 + 127, 0) - down, 1)
    scale = np.exp2(byte - 127.0)
    codes = (blocks / scale).astype(np.float32).astype(dtype).astype(np.float64)
    return np.moveaxis((codes * scale).reshape(v.shape), -1, axis)


WIDE = False


def mx_kscale(k):
    if not WIDE:
        return np.ones(k)
    levels = np.array([10, -10, 5, -5, 0])
    if k % 512:
        return np.exp2(np.random.permutation(np.resize(levels, k // 32))).repeat(32)
    a = np.empty((k // 512, 16))
    for p in range(k // 512):
        a[p, :8] = np.random.permutation(np.resize(levels, 8))
        for g in range(8):
            far = levels[np.abs(levels - a[p, g]) >= 10]
            a[p, g + 8] = far[np.random.randint(len(far))]
    return np.exp2(a.ravel()).repeat(32)


BF16 = ml_dtypes.bfloat16


def bf(x):
    return np.asarray(x, np.float32).astype(BF16)


def f64(x):
    return np.asarray(x).astype(np.float64)


T, H, I, R = 4096, 512, 128, 512


def silu(v):
    return v / (1.0 + np.exp(-v))


def draw0():
    s, t = mx_kscale(H), mx_kscale(R)
    return {
        "x": bf(np.random.standard_normal((T, H)) * s),
        "Wmean1": bf(np.random.standard_normal((I, H)) / np.sqrt(H) / s),
        "Wmean3": bf(np.random.standard_normal((I, H)) / np.sqrt(H) / s),
        "du1": bf(np.random.standard_normal((I, R)) * 0.5 / np.sqrt(R) / t),
        "dv1": bf(np.random.standard_normal((R, H)) / np.sqrt(H) / s * t[:, None]),
        "du3": bf(np.random.standard_normal((I, R)) * 0.5 / np.sqrt(R) / t),
        "dv3": bf(np.random.standard_normal((R, H)) / np.sqrt(H) / s * t[:, None]),
    }


def core(x, Wmean1, Wmean3, du1, dv1, du3, dv3):
    xq = mxq(f64(x), 1, "e4m3")
    p3 = xq @ mxq(f64(dv3), 1, "e4m3").T
    up = (xq @ mxq(f64(Wmean3), 1, "e4m3").T) + (mxq(p3, 1, "e4m3") @ mxq(f64(du3), 1, "e4m3").T)
    p1 = xq @ mxq(f64(dv1), 1, "e4m3").T
    gate = (xq @ mxq(f64(Wmean1), 1, "e4m3").T) + (mxq(p1, 1, "e4m3") @ mxq(f64(du1), 1, "e4m3").T)
    return silu(gate) * up


def e4m3fn_bytes(y):
    return np.clip(np.asarray(y, np.float64), -448.0, 448.0).astype(np.float32).astype(ml_dtypes.float8_e4m3fn).view(np.uint8)


def e4m3fn_values(b):
    return np.asarray(b, np.uint8).view(ml_dtypes.float8_e4m3fn).astype(np.float64)


def setup_inputs():
    d = draw0()
    x0 = np.asarray(d['x']).astype(np.float64)
    s = (np.max(np.abs(x0), axis=(0,), keepdims=True) / 448.0).astype(np.float32)
    out = {}
    for k, v in d.items():
        if k == 'x':
            out['x_bytes'] = e4m3fn_bytes(x0 / s.astype(np.float64))
            out['x_scale'] = s
        else:
            out[k] = v
    return out


def reference(x_bytes, x_scale, Wmean1, Wmean3, du1, dv1, du3, dv3):
    return core(e4m3fn_values(x_bytes) * x_scale.astype(np.float64), Wmean1, Wmean3, du1, dv1, du3, dv3)

@@ -1,0 +1,317 @@
+from contextlib import ExitStack
+
+import concourse.mybir as mybir
+from concourse.masks import make_identity
+
+TOKENS, FEATURES, OUT, INNER = 4096, 512, 128, 512
+FLOPS = 2 * TOKENS * (2 * FEATURES * INNER + 2 * FEATURES * OUT + 2 * INNER * OUT)
+
+F32 = mybir.dt.float32
+BF16 = mybir.dt.bfloat16
+U32 = mybir.dt.uint32
+U8 = mybir.dt.uint8
+FP8 = mybir.dt.float8_e4m3fn
+FP8X4 = mybir.dt.float8_e4m3fn_x4
+ACT = mybir.ActivationFunctionType
+MULT = mybir.AluOpType.mult
+
+P = 128
+PACK = 4
+SUPER = 512
+TILES = SUPER // P
+SUPERS = TOKENS // SUPER
+HALVES = 2 * SUPERS
+
+X_ON_VECTOR = {(g, 1) for g in range(1, SUPERS)} | {(g, 0) for g in (3, 5)}
+P_ON_VECTOR = {(13, 1, 1), (14, 0, 1), (14, 1, 1), (15, 0, 1), (15, 1, 1)}
+QXP = 0
+SII, SID, MUI, XI0, XI1, FMI, TRI = 1, 2, 2, 0, 1, 2, 1
+
+
+def tile_merge_mixtralsparsemoeblock_pa_t_kernel(tc, x_bytes, x_scale, Wmean1, Wmean3, du1, dv1, du3, dv3, out):
+    nc = tc.nc
+    x_view = x_bytes.rearrange("(g p a) k -> g p (a k)", p=P, a=TILES)
+    out_view = out.rearrange("(g p a) i -> g p a i", p=P, a=TILES)
+
+    with ExitStack() as ctx:
+        keep = ctx.enter_context(tc.tile_pool(name="keep", bufs=1))
+        xpool = ctx.enter_context(tc.tile_pool(name="xpool", bufs=3))
+        ppool = ctx.enter_context(tc.tile_pool(name="ppool", bufs=3))
+        psum_x = ctx.enter_context(tc.psum_pool(name="psum_x", bufs=2))
+        psum_p = ctx.enter_context(tc.psum_pool(name="psum_p", bufs=4))
+        psum_o = ctx.enter_context(tc.psum_pool(name="psum_o", bufs=1))
+        ctx.enter_context(tc.manual_schedule())
+
+        s_raw = keep.tile([P, PACK], F32, name="s_raw")
+        nc.sync.dma_start(out=s_raw[:], in_=x_scale.rearrange("o (p c) -> p (o c)", c=PACK))
+        xb_tiles = {}
+
+        def load_x(g, parts):
+            t = keep.tile([P, TILES * FEATURES], U8, name="x_raw%d" % g)
+            xb_tiles[g] = t
+            w = TILES * FEATURES // parts
+            for i in range(parts):
+                nc.sync.dma_start(out=t[:, i * w : (i + 1) * w], in_=x_view[g][:, i * w : (i + 1) * w])
+
+        def load_dv(src, name):
+            t = keep.tile([P, PACK, FEATURES], BF16, name=name)
+            v = src.rearrange("(m t) k -> m t k", t=PACK)
+            for i in range(2):
+                nc.sync.dma_start(out=t[:, 2 * i : 2 * i + 2, :], in_=v[:, 2 * i : 2 * i + 2, :])
+            return t
+
+        def load_pair(a, b, name):
+            t = keep.tile([P, 2, FEATURES], BF16, name=name)
+            nc.sync.dma_start(out=t[:, 0, :], in_=a)
+            nc.sync.dma_start(out=t[:, 1, :], in_=b)
+            return t
+
+        def part_x(t, g, lo, hi):
+            nc.sync.dma_start(out=t[:, lo * FEATURES : hi * FEATURES], in_=x_view[g][:, lo * FEATURES : hi * FEATURES])
+
+        x0 = keep.tile([P, TILES * FEATURES], U8, name="x_raw0")
+        xb_tiles[0] = x0
+        part_x(x0, 0, 0, 2)
+        dv1_raw = load_dv(dv1, "dv1_raw")
+        part_x(x0, 0, 2, 4)
+        dv3_raw = load_dv(dv3, "dv3_raw")
+        load_x(1, 1)
+        w_raw = load_pair(Wmean1, Wmean3, "w_raw")
+        du_raw = load_pair(du1, du3, "du_raw")
+        for g in range(2, SUPERS):
+            load_x(g, 1)
+
+        ident = keep.tile([P, P], F32, name="ident")
+        make_identity(nc, ident[:])
+        warm = keep.tile([P, 1], F32, name="warm")
+        nc.gpsimd.memset(warm[:], 0.0)
+        warm_out = keep.tile([P, 1], F32, name="warm_out")
+        nc.scalar.activation(out=warm_out[:], in_=warm[:], func=ACT.Silu)
+
+        s_ps = psum_p.tile([P, PACK, P], F32, name="s_ps", tag="pp")
+        for c in range(PACK):
+            nc.tensor.transpose(s_ps[:, c, :], s_raw[:, c : c + 1].to_broadcast([P, P]), ident[:])
+        scale = keep.tile([P, FEATURES], F32, name="scale")
+        nc.vector.tensor_copy(out=scale[:].rearrange("p (j c) -> p j c", c=PACK), in_=s_ps[:].rearrange("p c j -> p j c"))
+
+        def turn(bank, rows, words):
+            for row, w in zip(rows, words):
+                for u in range(2):
+                    nc.tensor.transpose(bank[:, row, u, :], w[:, u : FEATURES // 2 : 2], ident[:])
+
+        def untangle(copy, grouped, c0, bank):
+            dst = grouped.rearrange("p c t -> p (c t)").bitcast(F32)[:, 2 * c0 : 2 * c0 + 512]
+            copy(out=dst.rearrange("p (j m u) -> p j m u", j=2, u=2), in_=bank.rearrange("p j u m -> p j m u"))
+
+        def quantize(codes, scales, grouped):
+            nc.vector.quantize_mx(out=codes.bitcast(FP8X4), scales=scales, in_=grouped)
+
+        def weight_tiles(name, cols):
+            grouped = keep.tile([P, cols, PACK], BF16, name=name + "_g", align_bytes=64)
+            codes = keep.tile([P, cols], U32, name=name + "_c", align_bytes=64)
+            scales = keep.tile([P, cols], U8, name=name + "_s", align_bytes=64)
+            return grouped, codes, scales
+
+        def weight_turn(raw, grouped, b, pool, tag, copy, bankname):
+            bank = pool.tile([P, 2, 2, P], F32, name=bankname, tag=tag)
+            turn(bank, (0, 1), [raw[:, 2 * b + i, :].bitcast(F32) for i in range(2)])
+            if copy is not None:
+                untangle(copy, grouped[:], 2 * b * P, bank[:])
+            return bank
+
+        def flat(t):
+            return t[:].rearrange("p c t -> p (c t)")
+
+        prod, xg, xc, xs = {}, {}, {}, {}
+
+        def PR(g, a):
+            if g >= SUPERS:
+                return
+            if a == 0:
+                prod[g] = xpool.tile([P, TILES, FEATURES], BF16, name="x_bf%d" % g, tag="x_bf")
+            nc.vector.tensor_tensor(
+                out=prod[g][:, a, :],
+                in0=xb_tiles[g][:, a * FEATURES : (a + 1) * FEATURES].bitcast(FP8),
+                in1=scale[:],
+                op=MULT,
+            )
+
+        xbank = {}
+
+        def TR(g, b):
+            if g >= SUPERS:
+                return
+            xbank[g, b] = psum_x.tile([P, 2, 2, P], F32, name="xbank%d_%d" % (g, b), tag="xb")
+            turn(xbank[g, b], (0, 1), [prod[g][:, 2 * b + i, :].bitcast(F32) for i in range(2)])
+
+        def XE(g, b, copy):
+            if g >= SUPERS:
+                return
+            if b == 0:
+                xg[g] = xpool.tile([P, SUPER, PACK], BF16, name="x_g%d" % g, tag="x_g", align_bytes=64)
+            untangle(copy, xg[g][:], 2 * b * P, xbank[g, b][:])
+
+        def QX(g, lo, hi):
+            if g >= SUPERS:
+                return
+            if lo == 0:
+                xc[g] = xpool.tile([P, SUPER], U32, name="x_c%d" % g, tag="x_c", align_bytes=64)
+                xs[g] = xpool.tile([P, SUPER], U8, name="x_s%d" % g, tag="x_s", align_bytes=64)
+            quantize(xc[g][:, lo:hi], xs[g][:, lo:hi], flat(xg[g])[:, PACK * lo : PACK * hi])
+
+        pbank, pg, pc, psc = {}, {}, {}, {}
+
+        def PM(s, w, j):
+            g, h = divmod(s, 2)
+            bank = psum_p.tile([P, PACK, P], F32, name="pbank%d_%d_%d" % (s, w, j), tag="pp")
+            pbank[s, w, j] = bank
+            cols = slice((2 * h + j) * P, (2 * h + j + 1) * P)
+            grouped, codes, scales = dv[w]
+            for t in range(PACK):
+                nc.tensor.matmul_mx(
+                    out=bank[:, t, :],
+                    lhsT=codes[:, t * P : (t + 1) * P].bitcast(FP8X4),
+                    lhsT_scale=scales[:, t * P : (t + 1) * P],
+                    rhs=xc[g][:, cols].bitcast(FP8X4),
+                    rhs_scale=xs[g][:, cols],
+                    start=True,
+                    stop=True,
+                )
+
+        def PE(s, w, j, copy):
+            if j == 0:
+                pg[s, w] = ppool.tile([P, 2 * P, PACK], BF16, name="p_g%d_%d" % (s, w), tag="p_g%d" % w, align_bytes=64)
+            copy(out=pg[s, w][:, j * P : (j + 1) * P, :], in_=pbank[s, w, j][:].rearrange("p t n -> p n t"))
+
+        def QP(s, w):
+            if not 0 <= s < HALVES:
+                return
+            pc[s, w] = ppool.tile([P, 2 * P], U32, name="p_c%d_%d" % (s, w), tag="p_c%d" % w, align_bytes=64)
+            psc[s, w] = ppool.tile([P, 2 * P], U8, name="p_s%d_%d" % (s, w), tag="p_s%d" % w, align_bytes=64)
+            quantize(pc[s, w][:], psc[s, w][:], flat(pg[s, w]))
+
+        fin, sg, oo = {}, {}, {}
+
+        def FM(s):
+            if not 0 <= s < HALVES:
+                return
+            g, h = divmod(s, 2)
+            for w in range(2):
+                bank = psum_o.tile([P, 2, OUT], F32, name="fin%d_%d" % (s, w), tag="fin%d" % w)
+                fin[s, w] = bank
+                for j in range(2):
+                    xcols = slice((2 * h + j) * P, (2 * h + j + 1) * P)
+                    pcols = slice(j * P, (j + 1) * P)
+                    wcols = slice(w * OUT, (w + 1) * OUT)
+                    nc.tensor.matmul_mx(
+                        out=bank[:, j, :],
+                        lhsT=xc[g][:, xcols].bitcast(FP8X4),
+                        lhsT_scale=xs[g][:, xcols],
+                        rhs=wm[1][:, wcols].bitcast(FP8X4),
+                        rhs_scale=wm[2][:, wcols],
+                        start=True,
+                        stop=False,
+                    )
+                    nc.tensor.matmul_mx(
+                        out=bank[:, j, :],
+                        lhsT=pc[s, w][:, pcols].bitcast(FP8X4),
+                        lhsT_scale=psc[s, w][:, pcols],
+                        rhs=du[1][:, wcols].bitcast(FP8X4),
+                        rhs_scale=du[2][:, wcols],
+                        start=False,
+                        stop=True,
+                    )
+
+        def SI(s):
+            if not 0 <= s < HALVES:
+                return
+            sg[s] = ppool.tile([P, 2, OUT], F32, name="sg%d" % s, tag="sg")
+            nc.scalar.activation(out=sg[s][:], in_=fin[s, 0][:], func=ACT.Silu)
+
+        def MU(s):
+            if not 0 <= s < HALVES:
+                return
+            g, h = divmod(s, 2)
+            oo[s] = ppool.tile([P, 2, OUT], F32, name="oo%d" % s, tag="oo")
+            nc.vector.tensor_tensor(out=oo[s][:], in0=fin[s, 1][:], in1=sg[s][:], op=MULT)
+            nc.sync.dma_start(out=out_view[g][:, 2 * h : 2 * h + 2, :], in_=oo[s][:])
+
+        vcopy = nc.vector.tensor_copy
+        scopy = nc.scalar.copy
+
+        dv = [weight_tiles("dv1", INNER), weight_tiles("dv3", INNER)]
+        wm = weight_tiles("w", 2 * OUT)
+        du = weight_tiles("du", 2 * OUT)
+        BANKS = ((0, 0), (0, 1), (1, 0), (1, 1))
+
+        def pick(flag):
+            return vcopy if flag else scopy
+
+        PR(0, 0)
+        PR(0, 1)
+        for b in range(2):
+            weight_turn(dv1_raw, dv[0][0], b, psum_p, "pp", scopy, "dv1bank%d" % b)
+        TR(0, 0)
+        XE(0, 0, scopy)
+        quantize(dv[0][1][:], dv[0][2][:], flat(dv[0][0]))
+        PR(0, 2)
+        QX(0, 0, 2 * P)
+        for b in range(2):
+            weight_turn(dv3_raw, dv[1][0], b, psum_p, "pp", scopy, "dv3bank%d" % b)
+        PM(0, 0, 0)
+        PM(0, 0, 1)
+        PE(0, 0, 0, scopy)
+        PE(0, 0, 1, scopy)
+        PR(0, 3)
+        TR(0, 1)
+        quantize(dv[1][1][:], dv[1][2][:], flat(dv[1][0]))
+        XE(0, 1, scopy)
+        PM(0, 1, 0)
+        PM(0, 1, 1)
+        wbank = weight_turn(w_raw, wm[0], 0, psum_o, "fin0", None, "wbank")
+        dubank = weight_turn(du_raw, du[0], 0, psum_o, "fin1", None, "dubank")
+        PR(1, 0)
+        PR(1, 1)
+        QX(0, 2 * P, 4 * P)
+        PR(1, 2)
+        PR(1, 3)
+
+        for s in range(-1, HALVES + 2):
+            g, h = divmod(s, 2)
+            if s >= 0:
+                if h == 1 and QXP == 0:
+                    QX(g + 1, 0, SUPER)
+                QP(s - 1, 0)
+                if h == 1 and QXP == 1:
+                    QX(g + 1, 0, SUPER)
+                PR(g + 2, 2 * h)
+                if h == 1 and QXP == 2:
+                    QX(g + 1, 0, SUPER)
+                QP(s - 1, 1)
+            for i, (w, j) in enumerate(BANKS):
+                if (0 <= s < HALVES) and (s, w) != (0, 0):
+                    PE(s, w, j, pick((s, w, j) in P_ON_VECTOR))
+                if 0 <= s and s + 1 < HALVES:
+                    PM(s + 1, w, j)
+                if i == SII and s - SID >= 0:
+                    SI(s - SID)
+                if i == MUI and s - 2 >= 0:
+                    MU(s - 2)
+                if s == 0 and i == 0:
+                    untangle(scopy, wm[0][:], 0, wbank[:])
+                if s == 0 and i == 1:
+                    untangle(scopy, du[0][:], 0, dubank[:])
+                if s == 0 and i == 2:
+                    quantize(wm[1][:], wm[2][:], flat(wm[0]))
+                    quantize(du[1][:], du[2][:], flat(du[0]))
+                if h == 0 and i == XI0:
+                    XE(g + 1, 0, pick((g + 1, 0) in X_ON_VECTOR))
+                if i == 0 and s >= 0:
+                    PR(g + 2, 2 * h + 1)
+                if h == 0 and i == XI1:
+                    XE(g + 1, 1, pick((g + 1, 1) in X_ON_VECTOR))
+                if i == FMI:
+                    FM(s - 1)
+                if h == 1 and i == TRI:
+                    TR(g + 2, 0)
+                    TR(g + 2, 1)

@@ -22,10 +22,12 @@ TILES = SUPER // P
 SUPERS = TOKENS // SUPER
 HALVES = 2 * SUPERS
 
-X_ON_VECTOR = {(g, 1) for g in range(1, SUPERS)} | {(g, 0) for g in (3, 5)}
-P_ON_VECTOR = {(13, 1, 1), (14, 0, 1), (14, 1, 1), (15, 0, 1), (15, 1, 1)}
+X_ON_VECTOR = {(g, 1) for g in range(1, SUPERS)} | {(g, 0) for g in (3, 5, 7)}
+P_ON_VECTOR = {(13, 1, 0), (14, 1, 0), (14, 1, 1), (15, 1, 0), (15, 1, 1)}
+QPP = 1
+LASTM = 13
 QXP = 0
-SII, SID, MUI, XI0, XI1, FMI, TRI = 1, 2, 2, 0, 1, 2, 1
+SII, SID, MUI, XI0, XI1, FMI, TRI = 1, 2, 1, 0, 0, 2, 1
 
 
 def tile_merge_mixtralsparsemoeblock_pa_t_kernel(tc, x_bytes, x_scale, Wmean1, Wmean3, du1, dv1, du3, dv3, out):
@@ -91,8 +93,9 @@ def tile_merge_mixtralsparsemoeblock_pa_t_kernel(tc, x_bytes, x_scale, Wmean1, W
         s_ps = psum_p.tile([P, PACK, P], F32, name="s_ps", tag="pp")
         for c in range(PACK):
             nc.tensor.transpose(s_ps[:, c, :], s_raw[:, c : c + 1].to_broadcast([P, P]), ident[:])
-        scale = keep.tile([P, FEATURES], F32, name="scale")
-        nc.vector.tensor_copy(out=scale[:].rearrange("p (j c) -> p j c", c=PACK), in_=s_ps[:].rearrange("p c j -> p j c"))
+        scale = keep.tile([P, 2, FEATURES], F32, name="scale")
+        for i, copy in enumerate((nc.vector.tensor_copy, nc.scalar.copy)):
+            copy(out=scale[:, i, :].rearrange("p (j c) -> p j c", c=PACK), in_=s_ps[:].rearrange("p c j -> p j c"))
 
         def turn(bank, rows, words):
             for row, w in zip(rows, words):
@@ -124,15 +127,15 @@ def tile_merge_mixtralsparsemoeblock_pa_t_kernel(tc, x_bytes, x_scale, Wmean1, W
 
         prod, xg, xc, xs = {}, {}, {}, {}
 
-        def PR(g, a):
+        def PR(g, a, n=1):
             if g >= SUPERS:
                 return
             if a == 0:
                 prod[g] = xpool.tile([P, TILES, FEATURES], BF16, name="x_bf%d" % g, tag="x_bf")
             nc.vector.tensor_tensor(
-                out=prod[g][:, a, :],
-                in0=xb_tiles[g][:, a * FEATURES : (a + 1) * FEATURES].bitcast(FP8),
-                in1=scale[:],
+                out=prod[g][:, a : a + n, :].rearrange("p a k -> p (a k)"),
+                in0=xb_tiles[g][:, a * FEATURES : (a + n) * FEATURES].bitcast(FP8),
+                in1=scale[:, 0:n, :].rearrange("p a k -> p (a k)"),
                 op=MULT,
             )
 
@@ -179,32 +182,37 @@ def tile_merge_mixtralsparsemoeblock_pa_t_kernel(tc, x_bytes, x_scale, Wmean1, W
                 )
 
         def PE(s, w, j, copy):
-            if j == 0:
-                pg[s, w] = ppool.tile([P, 2 * P, PACK], BF16, name="p_g%d_%d" % (s, w), tag="p_g%d" % w, align_bytes=64)
-            copy(out=pg[s, w][:, j * P : (j + 1) * P, :], in_=pbank[s, w, j][:].rearrange("p t n -> p n t"))
+            if s not in pg:
+                pg[s] = ppool.tile([P, 2, 2, P, PACK], BF16, name="p_g%d" % s, tag="p_g", align_bytes=64)
+            copy(out=pg[s][:, j, w, :, :], in_=pbank[s, w, j][:].rearrange("p t n -> p n t"))
 
-        def QP(s, w):
+        def QP(s, j, n=1):
             if not 0 <= s < HALVES:
                 return
-            pc[s, w] = ppool.tile([P, 2 * P], U32, name="p_c%d_%d" % (s, w), tag="p_c%d" % w, align_bytes=64)
-            psc[s, w] = ppool.tile([P, 2 * P], U8, name="p_s%d_%d" % (s, w), tag="p_s%d" % w, align_bytes=64)
-            quantize(pc[s, w][:], psc[s, w][:], flat(pg[s, w]))
+            if j == 0:
+                pc[s] = ppool.tile([P, 2, 2, P], U32, name="p_c%d" % s, tag="p_c", align_bytes=64)
+                psc[s] = ppool.tile([P, 2, 2, P], U8, name="p_s%d" % s, tag="p_s", align_bytes=64)
+            quantize(
+                pc[s][:, j : j + n, :, :].rearrange("p j w c -> p (j w c)"),
+                psc[s][:, j : j + n, :, :].rearrange("p j w c -> p (j w c)"),
+                pg[s][:, j : j + n, :, :, :].rearrange("p j w c t -> p (j w c t)"),
+            )
 
         fin, sg, oo = {}, {}, {}
 
-        def FM(s):
+        def FM(s, j0=0, n=2, pool=psum_o, tag="fin%d"):
             if not 0 <= s < HALVES:
                 return
             g, h = divmod(s, 2)
             for w in range(2):
-                bank = psum_o.tile([P, 2, OUT], F32, name="fin%d_%d" % (s, w), tag="fin%d" % w)
-                fin[s, w] = bank
-                for j in range(2):
+                bank = pool.tile([P, n, OUT], F32, name="fin%d_%d_%d" % (s, w, j0), tag=tag % w if "%" in tag else tag)
+                fin[s, w, j0] = bank
+                for i in range(n):
+                    j = j0 + i
                     xcols = slice((2 * h + j) * P, (2 * h + j + 1) * P)
-                    pcols = slice(j * P, (j + 1) * P)
                     wcols = slice(w * OUT, (w + 1) * OUT)
                     nc.tensor.matmul_mx(
-                        out=bank[:, j, :],
+                        out=bank[:, i, :],
                         lhsT=xc[g][:, xcols].bitcast(FP8X4),
                         lhsT_scale=xs[g][:, xcols],
                         rhs=wm[1][:, wcols].bitcast(FP8X4),
@@ -213,28 +221,28 @@ def tile_merge_mixtralsparsemoeblock_pa_t_kernel(tc, x_bytes, x_scale, Wmean1, W
                         stop=False,
                     )
                     nc.tensor.matmul_mx(
-                        out=bank[:, j, :],
-                        lhsT=pc[s, w][:, pcols].bitcast(FP8X4),
-                        lhsT_scale=psc[s, w][:, pcols],
+                        out=bank[:, i, :],
+                        lhsT=pc[s][:, j, w, :].bitcast(FP8X4),
+                        lhsT_scale=psc[s][:, j, w, :],
                         rhs=du[1][:, wcols].bitcast(FP8X4),
                         rhs_scale=du[2][:, wcols],
                         start=False,
                         stop=True,
                     )
 
-        def SI(s):
+        def SI(s, j=0, n=2):
             if not 0 <= s < HALVES:
                 return
-            sg[s] = ppool.tile([P, 2, OUT], F32, name="sg%d" % s, tag="sg")
-            nc.scalar.activation(out=sg[s][:], in_=fin[s, 0][:], func=ACT.Silu)
+            sg[s, j] = ppool.tile([P, n, OUT], F32, name="sg%d_%d" % (s, j), tag="sg", bufs=4)
+            nc.scalar.activation(out=sg[s, j][:], in_=fin[s, 0, j][:], func=ACT.Silu)
 
-        def MU(s):
+        def MU(s, j=0, n=2):
             if not 0 <= s < HALVES:
                 return
             g, h = divmod(s, 2)
-            oo[s] = ppool.tile([P, 2, OUT], F32, name="oo%d" % s, tag="oo")
-            nc.vector.tensor_tensor(out=oo[s][:], in0=fin[s, 1][:], in1=sg[s][:], op=MULT)
-            nc.sync.dma_start(out=out_view[g][:, 2 * h : 2 * h + 2, :], in_=oo[s][:])
+            oo[s, j] = ppool.tile([P, n, OUT], F32, name="oo%d_%d" % (s, j), tag="oo", bufs=6)
+            nc.vector.tensor_tensor(out=oo[s, j][:], in0=fin[s, 1, j][:], in1=sg[s, j][:], op=MULT)
+            nc.sync.dma_start(out=out_view[g][:, 2 * h + j : 2 * h + j + n, :], in_=oo[s, j][:])
 
         vcopy = nc.vector.tensor_copy
         scopy = nc.scalar.copy
@@ -242,7 +250,8 @@ def tile_merge_mixtralsparsemoeblock_pa_t_kernel(tc, x_bytes, x_scale, Wmean1, W
         dv = [weight_tiles("dv1", INNER), weight_tiles("dv3", INNER)]
         wm = weight_tiles("w", 2 * OUT)
         du = weight_tiles("du", 2 * OUT)
-        BANKS = ((0, 0), (0, 1), (1, 0), (1, 1))
+        BANKS = ((0, 0), (1, 0), (0, 1), (1, 1))
+        HEADP = {(0, 0)}
 
         def pick(flag):
             return vcopy if flag else scopy
@@ -270,32 +279,39 @@ def tile_merge_mixtralsparsemoeblock_pa_t_kernel(tc, x_bytes, x_scale, Wmean1, W
         PM(0, 1, 1)
         wbank = weight_turn(w_raw, wm[0], 0, psum_o, "fin0", None, "wbank")
         dubank = weight_turn(du_raw, du[0], 0, psum_o, "fin1", None, "dubank")
-        PR(1, 0)
-        PR(1, 1)
+        PR(1, 0, 2)
         QX(0, 2 * P, 4 * P)
-        PR(1, 2)
-        PR(1, 3)
+        PR(1, 2, 2)
 
-        for s in range(-1, HALVES + 2):
+        LAST = HALVES - 1
+
+        def QPS(s):
+            if s < LASTM:
+                QP(s, 0, 2)
+            else:
+                QP(s, 0)
+                QP(s, 1)
+
+        for s in range(-1, HALVES):
             g, h = divmod(s, 2)
             if s >= 0:
+                if QPP == 0:
+                    QPS(s - 1)
                 if h == 1 and QXP == 0:
                     QX(g + 1, 0, SUPER)
-                QP(s - 1, 0)
+                PR(g + 2, 2 * h, 2)
+                if QPP == 1:
+                    QPS(s - 1)
                 if h == 1 and QXP == 1:
                     QX(g + 1, 0, SUPER)
-                PR(g + 2, 2 * h)
-                if h == 1 and QXP == 2:
-                    QX(g + 1, 0, SUPER)
-                QP(s - 1, 1)
             for i, (w, j) in enumerate(BANKS):
-                if (0 <= s < HALVES) and (s, w) != (0, 0):
+                if 0 <= s and (s, w) not in HEADP:
                     PE(s, w, j, pick((s, w, j) in P_ON_VECTOR))
                 if 0 <= s and s + 1 < HALVES:
                     PM(s + 1, w, j)
-                if i == SII and s - SID >= 0:
-                    SI(s - SID)
-                if i == MUI and s - 2 >= 0:
+                if i == SII:
+                    SI(s - 2)
+                if i == MUI:
                     MU(s - 2)
                 if s == 0 and i == 0:
                     untangle(scopy, wm[0][:], 0, wbank[:])
@@ -306,12 +322,22 @@ def tile_merge_mixtralsparsemoeblock_pa_t_kernel(tc, x_bytes, x_scale, Wmean1, W
                     quantize(du[1][:], du[2][:], flat(du[0]))
                 if h == 0 and i == XI0:
                     XE(g + 1, 0, pick((g + 1, 0) in X_ON_VECTOR))
-                if i == 0 and s >= 0:
-                    PR(g + 2, 2 * h + 1)
                 if h == 0 and i == XI1:
                     XE(g + 1, 1, pick((g + 1, 1) in X_ON_VECTOR))
-                if i == FMI:
+                if s == LAST and i == 1:
+                    FM(s - 1)
+                    QP(s, 0)
+                    FM(s, 0, 1, psum_x, "xb")
+                elif i == FMI and s < LAST:
                     FM(s - 1)
                 if h == 1 and i == TRI:
                     TR(g + 2, 0)
                     TR(g + 2, 1)
+        SI(LAST - 1)
+        MU(LAST - 1)
+        SI(LAST, 0, 1)
+        QP(LAST, 1)
+        MU(LAST, 0, 1)
+        FM(LAST, 1, 1)
+        SI(LAST, 1, 1)
+        MU(LAST, 1, 1)

@@ -22,8 +22,8 @@ TILES = SUPER // P
 SUPERS = TOKENS // SUPER
 HALVES = 2 * SUPERS
 
-X_ON_VECTOR = {(g, 1) for g in range(1, SUPERS)} | {(g, 0) for g in (3, 5, 7)}
-P_ON_VECTOR = {(13, 1, 0), (14, 1, 0), (14, 1, 1), (15, 1, 0), (15, 1, 1)}
+X_ON_VECTOR = [(1, 1), (2, 1), (3, 0), (4, 1), (5, 0), (5, 1), (6, 1), (7, 0), (7, 1)]
+P_ON_VECTOR = [(13, 1, 0), (14, 1, 0), (15, 1, 0), (15, 1, 1)]
 QPP = 1
 LASTM = 13
 QXP = 0
@@ -45,7 +45,6 @@ def tile_merge_mixtralsparsemoeblock_pa_t_kernel(tc, x_bytes, x_scale, Wmean1, W
         ctx.enter_context(tc.manual_schedule())
 
         s_raw = keep.tile([P, PACK], F32, name="s_raw")
-        nc.sync.dma_start(out=s_raw[:], in_=x_scale.rearrange("o (p c) -> p (o c)", c=PACK))
         xb_tiles = {}
 
         def load_x(g, parts):
@@ -55,31 +54,32 @@ def tile_merge_mixtralsparsemoeblock_pa_t_kernel(tc, x_bytes, x_scale, Wmean1, W
             for i in range(parts):
                 nc.sync.dma_start(out=t[:, i * w : (i + 1) * w], in_=x_view[g][:, i * w : (i + 1) * w])
 
-        def load_dv(src, name):
-            t = keep.tile([P, PACK, FEATURES], BF16, name=name)
-            v = src.rearrange("(m t) k -> m t k", t=PACK)
-            for i in range(2):
-                nc.sync.dma_start(out=t[:, 2 * i : 2 * i + 2, :], in_=v[:, 2 * i : 2 * i + 2, :])
-            return t
-
-        def load_pair(a, b, name):
-            t = keep.tile([P, 2, FEATURES], BF16, name=name)
-            nc.sync.dma_start(out=t[:, 0, :], in_=a)
-            nc.sync.dma_start(out=t[:, 1, :], in_=b)
-            return t
-
         def part_x(t, g, lo, hi):
             nc.sync.dma_start(out=t[:, lo * FEATURES : hi * FEATURES], in_=x_view[g][:, lo * FEATURES : hi * FEATURES])
 
         x0 = keep.tile([P, TILES * FEATURES], U8, name="x_raw0")
         xb_tiles[0] = x0
+        dv1_raw = keep.tile([P, PACK, FEATURES], BF16, name="dv1_raw")
+        dv3_raw = keep.tile([P, PACK, FEATURES], BF16, name="dv3_raw")
+        w_raw = keep.tile([P, 2, FEATURES], BF16, name="w_raw")
+        du_raw = keep.tile([P, 2, FEATURES], BF16, name="du_raw")
+
+        def load_slots(tile, src, i):
+            v = src.rearrange("(m t) k -> m t k", t=PACK)
+            nc.sync.dma_start(out=tile[:, 2 * i : 2 * i + 2, :], in_=v[:, 2 * i : 2 * i + 2, :])
+
+        nc.sync.dma_start(out=s_raw[:], in_=x_scale.rearrange("o (p c) -> p (o c)", c=PACK))
         part_x(x0, 0, 0, 2)
-        dv1_raw = load_dv(dv1, "dv1_raw")
         part_x(x0, 0, 2, 4)
-        dv3_raw = load_dv(dv3, "dv3_raw")
+        load_slots(dv1_raw, dv1, 0)
+        load_slots(dv1_raw, dv1, 1)
+        nc.sync.dma_start(out=du_raw[:, 1, :], in_=du3)
+        load_slots(dv3_raw, dv3, 0)
+        nc.sync.dma_start(out=du_raw[:, 0, :], in_=du1)
+        load_slots(dv3_raw, dv3, 1)
+        nc.sync.dma_start(out=w_raw[:, 0, :], in_=Wmean1)
+        nc.sync.dma_start(out=w_raw[:, 1, :], in_=Wmean3)
         load_x(1, 1)
-        w_raw = load_pair(Wmean1, Wmean3, "w_raw")
-        du_raw = load_pair(du1, du3, "du_raw")
         for g in range(2, SUPERS):
             load_x(g, 1)
 
@@ -90,12 +90,17 @@ def tile_merge_mixtralsparsemoeblock_pa_t_kernel(tc, x_bytes, x_scale, Wmean1, W
         warm_out = keep.tile([P, 1], F32, name="warm_out")
         nc.scalar.activation(out=warm_out[:], in_=warm[:], func=ACT.Silu)
 
-        s_ps = psum_p.tile([P, PACK, P], F32, name="s_ps", tag="pp")
-        for c in range(PACK):
-            nc.tensor.transpose(s_ps[:, c, :], s_raw[:, c : c + 1].to_broadcast([P, P]), ident[:])
         scale = keep.tile([P, 2, FEATURES], F32, name="scale")
-        for i, copy in enumerate((nc.vector.tensor_copy, nc.scalar.copy)):
-            copy(out=scale[:, i, :].rearrange("p (j c) -> p j c", c=PACK), in_=s_ps[:].rearrange("p c j -> p j c"))
+        s_bank = []
+
+        def scale_turn():
+            s_ps = psum_p.tile([P, PACK, P], F32, name="s_ps", tag="pp")
+            s_bank.append(s_ps)
+            for c in range(PACK):
+                nc.tensor.transpose(s_ps[:, c, :], s_raw[:, c : c + 1].to_broadcast([P, P]), ident[:])
+
+        def scale_evac(i, copy):
+            copy(out=scale[:, i, :].rearrange("p (j c) -> p j c", c=PACK), in_=s_bank[0][:].rearrange("p c j -> p j c"))
 
         def turn(bank, rows, words):
             for row, w in zip(rows, words):
@@ -115,12 +120,18 @@ def tile_merge_mixtralsparsemoeblock_pa_t_kernel(tc, x_bytes, x_scale, Wmean1, W
             scales = keep.tile([P, cols], U8, name=name + "_s", align_bytes=64)
             return grouped, codes, scales
 
-        def weight_turn(raw, grouped, b, pool, tag, copy, bankname):
-            bank = pool.tile([P, 2, 2, P], F32, name=bankname, tag=tag)
+        wbanks = {}
+
+        def weight_turn(raw, b, pool, tag, name):
+            bank = pool.tile([P, 2, 2, P], F32, name="%sbank%d" % (name, b), tag=tag)
+            wbanks[name, b] = bank
             turn(bank, (0, 1), [raw[:, 2 * b + i, :].bitcast(F32) for i in range(2)])
-            if copy is not None:
-                untangle(copy, grouped[:], 2 * b * P, bank[:])
-            return bank
+
+        def weight_evac(name, b, grouped, copy):
+            untangle(copy, grouped[:], 2 * b * P, wbanks[name, b][:])
+
+        def quantize_weights(tiles):
+            quantize(tiles[1][:], tiles[2][:], flat(tiles[0]))
 
         def flat(t):
             return t[:].rearrange("p c t -> p (c t)")
@@ -138,6 +149,23 @@ def tile_merge_mixtralsparsemoeblock_pa_t_kernel(tc, x_bytes, x_scale, Wmean1, W
                 in1=scale[:, 0:n, :].rearrange("p a k -> p (a k)"),
                 op=MULT,
             )
+
+        def CAST(a):
+            if a == 0:
+                prod[0] = xpool.tile([P, TILES, FEATURES], BF16, name="x_bf0", tag="x_bf")
+            nc.vector.tensor_copy(out=prod[0][:, a, :], in_=x0[:, a * FEATURES : (a + 1) * FEATURES].bitcast(FP8))
+
+        def XP(b):
+            if b == 0:
+                xg[0] = xpool.tile([P, SUPER, PACK], BF16, name="x_g0", tag="x_g", align_bytes=64)
+            for j in range(2):
+                a = 2 * b + j
+                nc.vector.tensor_tensor(
+                    out=xg[0][:, a * P : (a + 1) * P, :].rearrange("p m (u e) -> p m u e", e=2),
+                    in0=xbank[0, b][:, j, :, :].bitcast(BF16).rearrange("p u (m e) -> p m u e", e=2),
+                    in1=s_raw[:].rearrange("p (o u e) -> p o u e", o=1, e=2).to_broadcast([P, P, 2, 2]),
+                    op=MULT,
+                )
 
         xbank = {}
 
@@ -256,32 +284,41 @@ def tile_merge_mixtralsparsemoeblock_pa_t_kernel(tc, x_bytes, x_scale, Wmean1, W
         def pick(flag):
             return vcopy if flag else scopy
 
-        PR(0, 0)
-        PR(0, 1)
-        for b in range(2):
-            weight_turn(dv1_raw, dv[0][0], b, psum_p, "pp", scopy, "dv1bank%d" % b)
+        CAST(0)
+        CAST(1)
+        scale_turn()
         TR(0, 0)
-        XE(0, 0, scopy)
-        quantize(dv[0][1][:], dv[0][2][:], flat(dv[0][0]))
-        PR(0, 2)
-        QX(0, 0, 2 * P)
-        for b in range(2):
-            weight_turn(dv3_raw, dv[1][0], b, psum_p, "pp", scopy, "dv3bank%d" % b)
-        PM(0, 0, 0)
-        PM(0, 0, 1)
-        PE(0, 0, 0, scopy)
-        PE(0, 0, 1, scopy)
-        PR(0, 3)
+        scale_evac(0, scopy)
+        CAST(2)
+        weight_turn(dv1_raw, 0, psum_p, "pp", "dv1")
+        CAST(3)
         TR(0, 1)
-        quantize(dv[1][1][:], dv[1][2][:], flat(dv[1][0]))
-        XE(0, 1, scopy)
+        weight_turn(dv1_raw, 1, psum_p, "pp", "dv1")
+        weight_evac("dv1", 0, dv[0][0], scopy)
+        weight_turn(dv3_raw, 0, psum_p, "pp", "dv3")
+        XP(0)
+        weight_turn(du_raw, 0, psum_o, "fin1", "du")
+        XP(1)
+        weight_evac("dv1", 1, dv[0][0], scopy)
+        quantize_weights(dv[0])
+        scale_evac(1, scopy)
+        weight_evac("dv3", 0, dv[1][0], scopy)
+        QX(0, 0, 2 * P)
+        weight_turn(w_raw, 0, psum_o, "fin0", "w")
+        weight_turn(dv3_raw, 1, psum_p, "pp", "dv3")
+        PM(0, 0, 0)
+        weight_evac("dv3", 1, dv[1][0], scopy)
+        QX(0, 2 * P, 4 * P)
+        PR(1, 0, 2)
+        quantize_weights(dv[1])
+        PR(1, 2, 2)
+        PM(0, 0, 1)
+        weight_evac("du", 0, du[0], scopy)
         PM(0, 1, 0)
         PM(0, 1, 1)
-        wbank = weight_turn(w_raw, wm[0], 0, psum_o, "fin0", None, "wbank")
-        dubank = weight_turn(du_raw, du[0], 0, psum_o, "fin1", None, "dubank")
-        PR(1, 0, 2)
-        QX(0, 2 * P, 4 * P)
-        PR(1, 2, 2)
+        weight_evac("w", 0, wm[0], scopy)
+        PE(0, 0, 0, scopy)
+        PE(0, 0, 1, scopy)
 
         LAST = HALVES - 1
 
@@ -313,13 +350,9 @@ def tile_merge_mixtralsparsemoeblock_pa_t_kernel(tc, x_bytes, x_scale, Wmean1, W
                     SI(s - 2)
                 if i == MUI:
                     MU(s - 2)
-                if s == 0 and i == 0:
-                    untangle(scopy, wm[0][:], 0, wbank[:])
-                if s == 0 and i == 1:
-                    untangle(scopy, du[0][:], 0, dubank[:])
                 if s == 0 and i == 2:
-                    quantize(wm[1][:], wm[2][:], flat(wm[0]))
-                    quantize(du[1][:], du[2][:], flat(du[0]))
+                    quantize_weights(wm)
+                    quantize_weights(du)
                 if h == 0 and i == XI0:
                     XE(g + 1, 0, pick((g + 1, 0) in X_ON_VECTOR))
                 if h == 0 and i == XI1:

from contextlib import ExitStack

import concourse.mybir as mybir
from concourse.masks import make_identity

TOKENS, FEATURES, OUT, INNER = 4096, 512, 128, 512
FLOPS = 2 * TOKENS * (2 * FEATURES * INNER + 2 * FEATURES * OUT + 2 * INNER * OUT)

F32 = mybir.dt.float32
BF16 = mybir.dt.bfloat16
U32 = mybir.dt.uint32
U8 = mybir.dt.uint8
FP8 = mybir.dt.float8_e4m3fn
FP8X4 = mybir.dt.float8_e4m3fn_x4
ACT = mybir.ActivationFunctionType
MULT = mybir.AluOpType.mult

P = 128
PACK = 4
SUPER = 512
TILES = SUPER // P
SUPERS = TOKENS // SUPER
HALVES = 2 * SUPERS

X_ON_VECTOR = [(1, 1), (2, 1), (3, 0), (4, 1), (5, 0), (5, 1), (6, 1), (7, 0), (7, 1)]
P_ON_VECTOR = [(13, 1, 0), (14, 1, 0), (15, 1, 0), (15, 1, 1)]
QPP = 1
LASTM = 13
QXP = 0
SII, SID, MUI, XI0, XI1, FMI, TRI = 1, 2, 1, 0, 0, 2, 1


def tile_merge_mixtralsparsemoeblock_pa_t_kernel(tc, x_bytes, x_scale, Wmean1, Wmean3, du1, dv1, du3, dv3, out):
    nc = tc.nc
    x_view = x_bytes.rearrange("(g p a) k -> g p (a k)", p=P, a=TILES)
    out_view = out.rearrange("(g p a) i -> g p a i", p=P, a=TILES)

    with ExitStack() as ctx:
        keep = ctx.enter_context(tc.tile_pool(name="keep", bufs=1))
        xpool = ctx.enter_context(tc.tile_pool(name="xpool", bufs=3))
        ppool = ctx.enter_context(tc.tile_pool(name="ppool", bufs=3))
        psum_x = ctx.enter_context(tc.psum_pool(name="psum_x", bufs=2))
        psum_p = ctx.enter_context(tc.psum_pool(name="psum_p", bufs=4))
        psum_o = ctx.enter_context(tc.psum_pool(name="psum_o", bufs=1))
        ctx.enter_context(tc.manual_schedule())

        s_raw = keep.tile([P, PACK], F32, name="s_raw")
        xb_tiles = {}

        def load_x(g, parts):
            t = keep.tile([P, TILES * FEATURES], U8, name="x_raw%d" % g)
            xb_tiles[g] = t
            w = TILES * FEATURES // parts
            for i in range(parts):
                nc.sync.dma_start(out=t[:, i * w : (i + 1) * w], in_=x_view[g][:, i * w : (i + 1) * w])

        def part_x(t, g, lo, hi):
            nc.sync.dma_start(out=t[:, lo * FEATURES : hi * FEATURES], in_=x_view[g][:, lo * FEATURES : hi * FEATURES])

        x0 = keep.tile([P, TILES * FEATURES], U8, name="x_raw0")
        xb_tiles[0] = x0
        dv1_raw = keep.tile([P, PACK, FEATURES], BF16, name="dv1_raw")
        dv3_raw = keep.tile([P, PACK, FEATURES], BF16, name="dv3_raw")
        w_raw = keep.tile([P, 2, FEATURES], BF16, name="w_raw")
        du_raw = keep.tile([P, 2, FEATURES], BF16, name="du_raw")

        def load_slots(tile, src, i):
            v = src.rearrange("(m t) k -> m t k", t=PACK)
            nc.sync.dma_start(out=tile[:, 2 * i : 2 * i + 2, :], in_=v[:, 2 * i : 2 * i + 2, :])

        nc.sync.dma_start(out=s_raw[:], in_=x_scale.rearrange("o (p c) -> p (o c)", c=PACK))
        part_x(x0, 0, 0, 2)
        part_x(x0, 0, 2, 4)
        load_slots(dv1_raw, dv1, 0)
        load_slots(dv1_raw, dv1, 1)
        nc.sync.dma_start(out=du_raw[:, 1, :], in_=du3)
        load_slots(dv3_raw, dv3, 0)
        nc.sync.dma_start(out=du_raw[:, 0, :], in_=du1)
        load_slots(dv3_raw, dv3, 1)
        nc.sync.dma_start(out=w_raw[:, 0, :], in_=Wmean1)
        nc.sync.dma_start(out=w_raw[:, 1, :], in_=Wmean3)
        load_x(1, 1)
        for g in range(2, SUPERS):
            load_x(g, 1)

        ident = keep.tile([P, P], F32, name="ident")
        make_identity(nc, ident[:])
        warm = keep.tile([P, 1], F32, name="warm")
        nc.gpsimd.memset(warm[:], 0.0)
        warm_out = keep.tile([P, 1], F32, name="warm_out")
        nc.scalar.activation(out=warm_out[:], in_=warm[:], func=ACT.Silu)

        scale = keep.tile([P, 2, FEATURES], F32, name="scale")
        s_bank = []

        def scale_turn():
            s_ps = psum_p.tile([P, PACK, P], F32, name="s_ps", tag="pp")
            s_bank.append(s_ps)
            for c in range(PACK):
                nc.tensor.transpose(s_ps[:, c, :], s_raw[:, c : c + 1].to_broadcast([P, P]), ident[:])

        def scale_evac(i, copy):
            copy(out=scale[:, i, :].rearrange("p (j c) -> p j c", c=PACK), in_=s_bank[0][:].rearrange("p c j -> p j c"))

        def turn(bank, rows, words):
            for row, w in zip(rows, words):
                for u in range(2):
                    nc.tensor.transpose(bank[:, row, u, :], w[:, u : FEATURES // 2 : 2], ident[:])

        def untangle(copy, grouped, c0, bank):
            dst = grouped.rearrange("p c t -> p (c t)").bitcast(F32)[:, 2 * c0 : 2 * c0 + 512]
            copy(out=dst.rearrange("p (j m u) -> p j m u", j=2, u=2), in_=bank.rearrange("p j u m -> p j m u"))

        def quantize(codes, scales, grouped):
            nc.vector.quantize_mx(out=codes.bitcast(FP8X4), scales=scales, in_=grouped)

        def weight_tiles(name, cols):
            grouped = keep.tile([P, cols, PACK], BF16, name=name + "_g", align_bytes=64)
            codes = keep.tile([P, cols], U32, name=name + "_c", align_bytes=64)
            scales = keep.tile([P, cols], U8, name=name + "_s", align_bytes=64)
            return grouped, codes, scales

        wbanks = {}

        def weight_turn(raw, b, pool, tag, name):
            bank = pool.tile([P, 2, 2, P], F32, name="%sbank%d" % (name, b), tag=tag)
            wbanks[name, b] = bank
            turn(bank, (0, 1), [raw[:, 2 * b + i, :].bitcast(F32) for i in range(2)])

        def weight_evac(name, b, grouped, copy):
            untangle(copy, grouped[:], 2 * b * P, wbanks[name, b][:])

        def quantize_weights(tiles):
            quantize(tiles[1][:], tiles[2][:], flat(tiles[0]))

        def flat(t):
            return t[:].rearrange("p c t -> p (c t)")

        prod, xg, xc, xs = {}, {}, {}, {}

        def PR(g, a, n=1):
            if g >= SUPERS:
                return
            if a == 0:
                prod[g] = xpool.tile([P, TILES, FEATURES], BF16, name="x_bf%d" % g, tag="x_bf")
            nc.vector.tensor_tensor(
                out=prod[g][:, a : a + n, :].rearrange("p a k -> p (a k)"),
                in0=xb_tiles[g][:, a * FEATURES : (a + n) * FEATURES].bitcast(FP8),
                in1=scale[:, 0:n, :].rearrange("p a k -> p (a k)"),
                op=MULT,
            )

        def CAST(a):
            if a == 0:
                prod[0] = xpool.tile([P, TILES, FEATURES], BF16, name="x_bf0", tag="x_bf")
            nc.vector.tensor_copy(out=prod[0][:, a, :], in_=x0[:, a * FEATURES : (a + 1) * FEATURES].bitcast(FP8))

        def XP(b):
            if b == 0:
                xg[0] = xpool.tile([P, SUPER, PACK], BF16, name="x_g0", tag="x_g", align_bytes=64)
            for j in range(2):
                a = 2 * b + j
                nc.vector.tensor_tensor(
                    out=xg[0][:, a * P : (a + 1) * P, :].rearrange("p m (u e) -> p m u e", e=2),
                    in0=xbank[0, b][:, j, :, :].bitcast(BF16).rearrange("p u (m e) -> p m u e", e=2),
                    in1=s_raw[:].rearrange("p (o u e) -> p o u e", o=1, e=2).to_broadcast([P, P, 2, 2]),
                    op=MULT,
                )

        xbank = {}

        def TR(g, b):
            if g >= SUPERS:
                return
            xbank[g, b] = psum_x.tile([P, 2, 2, P], F32, name="xbank%d_%d" % (g, b), tag="xb")
            turn(xbank[g, b], (0, 1), [prod[g][:, 2 * b + i, :].bitcast(F32) for i in range(2)])

        def XE(g, b, copy):
            if g >= SUPERS:
                return
            if b == 0:
                xg[g] = xpool.tile([P, SUPER, PACK], BF16, name="x_g%d" % g, tag="x_g", align_bytes=64)
            untangle(copy, xg[g][:], 2 * b * P, xbank[g, b][:])

        def QX(g, lo, hi):
            if g >= SUPERS:
                return
            if lo == 0:
                xc[g] = xpool.tile([P, SUPER], U32, name="x_c%d" % g, tag="x_c", align_bytes=64)
                xs[g] = xpool.tile([P, SUPER], U8, name="x_s%d" % g, tag="x_s", align_bytes=64)
            quantize(xc[g][:, lo:hi], xs[g][:, lo:hi], flat(xg[g])[:, PACK * lo : PACK * hi])

        pbank, pg, pc, psc = {}, {}, {}, {}

        def PM(s, w, j):
            g, h = divmod(s, 2)
            bank = psum_p.tile([P, PACK, P], F32, name="pbank%d_%d_%d" % (s, w, j), tag="pp")
            pbank[s, w, j] = bank
            cols = slice((2 * h + j) * P, (2 * h + j + 1) * P)
            grouped, codes, scales = dv[w]
            for t in range(PACK):
                nc.tensor.matmul_mx(
                    out=bank[:, t, :],
                    lhsT=codes[:, t * P : (t + 1) * P].bitcast(FP8X4),
                    lhsT_scale=scales[:, t * P : (t + 1) * P],
                    rhs=xc[g][:, cols].bitcast(FP8X4),
                    rhs_scale=xs[g][:, cols],
                    start=True,
                    stop=True,
                )

        def PE(s, w, j, copy):
            if s not in pg:
                pg[s] = ppool.tile([P, 2, 2, P, PACK], BF16, name="p_g%d" % s, tag="p_g", align_bytes=64)
            copy(out=pg[s][:, j, w, :, :], in_=pbank[s, w, j][:].rearrange("p t n -> p n t"))

        def QP(s, j, n=1):
            if not 0 <= s < HALVES:
                return
            if j == 0:
                pc[s] = ppool.tile([P, 2, 2, P], U32, name="p_c%d" % s, tag="p_c", align_bytes=64)
                psc[s] = ppool.tile([P, 2, 2, P], U8, name="p_s%d" % s, tag="p_s", align_bytes=64)
            quantize(
                pc[s][:, j : j + n, :, :].rearrange("p j w c -> p (j w c)"),
                psc[s][:, j : j + n, :, :].rearrange("p j w c -> p (j w c)"),
                pg[s][:, j : j + n, :, :, :].rearrange("p j w c t -> p (j w c t)"),
            )

        fin, sg, oo = {}, {}, {}

        def FM(s, j0=0, n=2, pool=psum_o, tag="fin%d"):
            if not 0 <= s < HALVES:
                return
            g, h = divmod(s, 2)
            for w in range(2):
                bank = pool.tile([P, n, OUT], F32, name="fin%d_%d_%d" % (s, w, j0), tag=tag % w if "%" in tag else tag)
                fin[s, w, j0] = bank
                for i in range(n):
                    j = j0 + i
                    xcols = slice((2 * h + j) * P, (2 * h + j + 1) * P)
                    wcols = slice(w * OUT, (w + 1) * OUT)
                    nc.tensor.matmul_mx(
                        out=bank[:, i, :],
                        lhsT=xc[g][:, xcols].bitcast(FP8X4),
                        lhsT_scale=xs[g][:, xcols],
                        rhs=wm[1][:, wcols].bitcast(FP8X4),
                        rhs_scale=wm[2][:, wcols],
                        start=True,
                        stop=False,
                    )
                    nc.tensor.matmul_mx(
                        out=bank[:, i, :],
                        lhsT=pc[s][:, j, w, :].bitcast(FP8X4),
                        lhsT_scale=psc[s][:, j, w, :],
                        rhs=du[1][:, wcols].bitcast(FP8X4),
                        rhs_scale=du[2][:, wcols],
                        start=False,
                        stop=True,
                    )

        def SI(s, j=0, n=2):
            if not 0 <= s < HALVES:
                return
            sg[s, j] = ppool.tile([P, n, OUT], F32, name="sg%d_%d" % (s, j), tag="sg", bufs=4)
            nc.scalar.activation(out=sg[s, j][:], in_=fin[s, 0, j][:], func=ACT.Silu)

        def MU(s, j=0, n=2):
            if not 0 <= s < HALVES:
                return
            g, h = divmod(s, 2)
            oo[s, j] = ppool.tile([P, n, OUT], F32, name="oo%d_%d" % (s, j), tag="oo", bufs=6)
            nc.vector.tensor_tensor(out=oo[s, j][:], in0=fin[s, 1, j][:], in1=sg[s, j][:], op=MULT)
            nc.sync.dma_start(out=out_view[g][:, 2 * h + j : 2 * h + j + n, :], in_=oo[s, j][:])

        vcopy = nc.vector.tensor_copy
        scopy = nc.scalar.copy

        dv = [weight_tiles("dv1", INNER), weight_tiles("dv3", INNER)]
        wm = weight_tiles("w", 2 * OUT)
        du = weight_tiles("du", 2 * OUT)
        BANKS = ((0, 0), (1, 0), (0, 1), (1, 1))
        HEADP = {(0, 0)}

        def pick(flag):
            return vcopy if flag else scopy

        CAST(0)
        CAST(1)
        scale_turn()
        TR(0, 0)
        scale_evac(0, scopy)
        CAST(2)
        weight_turn(dv1_raw, 0, psum_p, "pp", "dv1")
        CAST(3)
        TR(0, 1)
        weight_turn(dv1_raw, 1, psum_p, "pp", "dv1")
        weight_evac("dv1", 0, dv[0][0], scopy)
        weight_turn(dv3_raw, 0, psum_p, "pp", "dv3")
        XP(0)
        weight_turn(du_raw, 0, psum_o, "fin1", "du")
        XP(1)
        weight_evac("dv1", 1, dv[0][0], scopy)
        quantize_weights(dv[0])
        scale_evac(1, scopy)
        weight_evac("dv3", 0, dv[1][0], scopy)
        QX(0, 0, 2 * P)
        weight_turn(w_raw, 0, psum_o, "fin0", "w")
        weight_turn(dv3_raw, 1, psum_p, "pp", "dv3")
        PM(0, 0, 0)
        weight_evac("dv3", 1, dv[1][0], scopy)
        QX(0, 2 * P, 4 * P)
        PR(1, 0, 2)
        quantize_weights(dv[1])
        PR(1, 2, 2)
        PM(0, 0, 1)
        weight_evac("du", 0, du[0], scopy)
        PM(0, 1, 0)
        PM(0, 1, 1)
        weight_evac("w", 0, wm[0], scopy)
        PE(0, 0, 0, scopy)
        PE(0, 0, 1, scopy)

        LAST = HALVES - 1

        def QPS(s):
            if s < LASTM:
                QP(s, 0, 2)
            else:
                QP(s, 0)
                QP(s, 1)

        for s in range(-1, HALVES):
            g, h = divmod(s, 2)
            if s >= 0:
                if QPP == 0:
                    QPS(s - 1)
                if h == 1 and QXP == 0:
                    QX(g + 1, 0, SUPER)
                PR(g + 2, 2 * h, 2)
                if QPP == 1:
                    QPS(s - 1)
                if h == 1 and QXP == 1:
                    QX(g + 1, 0, SUPER)
            for i, (w, j) in enumerate(BANKS):
                if 0 <= s and (s, w) not in HEADP:
                    PE(s, w, j, pick((s, w, j) in P_ON_VECTOR))
                if 0 <= s and s + 1 < HALVES:
                    PM(s + 1, w, j)
                if i == SII:
                    SI(s - 2)
                if i == MUI:
                    MU(s - 2)
                if s == 0 and i == 2:
                    quantize_weights(wm)
                    quantize_weights(du)
                if h == 0 and i == XI0:
                    XE(g + 1, 0, pick((g + 1, 0) in X_ON_VECTOR))
                if h == 0 and i == XI1:
                    XE(g + 1, 1, pick((g + 1, 1) in X_ON_VECTOR))
                if s == LAST and i == 1:
                    FM(s - 1)
                    QP(s, 0)
                    FM(s, 0, 1, psum_x, "xb")
                elif i == FMI and s < LAST:
                    FM(s - 1)
                if h == 1 and i == TRI:
                    TR(g + 2, 0)
                    TR(g + 2, 1)
        SI(LAST - 1)
        MU(LAST - 1)
        SI(LAST, 0, 1)
        QP(LAST, 1)
        MU(LAST, 0, 1)
        FM(LAST, 1, 1)
        SI(LAST, 1, 1)
        MU(LAST, 1, 1)
